import numpy as np
import ml_dtypes


def mxq(x, axis, fmt="e4m3"):
    dtype, down = {"e4m3": (ml_dtypes.float8_e4m3fn, 7), "e5m2": (ml_dtypes.float8_e5m2, 14)}[fmt]
    v = np.moveaxis(np.asarray(x, np.float32).astype(ml_dtypes.bfloat16).astype(np.float64), axis, -1)
    blocks = v.reshape(v.shape[:-1] + (-1, 32))
    amax = np.abs(blocks).max(-1, keepdims=True)
    byte = np.maximum(np.where(amax > 0, np.frexp(amax)[1] - 1 + 127, 0) - down, 1)
    scale = np.exp2(byte - 127.0)
    codes = (blocks / scale).astype(np.float32).astype(dtype).astype(np.float64)
    return np.moveaxis((codes * scale).reshape(v.shape), -1, axis)


WIDE = False


def mx_kscale(k):
    if not WIDE:
        return np.ones(k)
    levels = np.array([10, -10, 5, -5, 0])
    a = np.random.permutation(np.resize(levels, k // 512 * 4)).reshape(k // 512, 4)
    idx = np.arange(k)
    return np.exp2(a[idx // 512, idx % 128 // 32])


BF16 = ml_dtypes.bfloat16


def bf(x):
    return np.asarray(x, np.float32).astype(BF16)


def f64(x):
    return np.asarray(x).astype(np.float64)


E2M1 = np.array([0.0, 0.5, 1.0, 1.5, 2.0, 3.0, 4.0, 6.0, -0.0, -0.5, -1.0, -1.5, -2.0, -3.0, -4.0, -6.0])


def pack_weight(w, fmt):
    k, n = w.shape
    w = f64(bf(w)).reshape(k // 32, 32, n)
    amax = np.abs(w).max(1)
    if fmt == "e4m3":
        byte = np.frexp(amax)[1] - 1 + 127 - 7
    else:
        mant, ex = np.frexp(amax / 6.0)
        byte = np.where(mant > 0.5, ex, ex - 1) + 127
    byte = np.clip(np.where(amax > 0, byte, 1), 1, 254)
    scaled = (w * np.exp2(127.0 - byte)[:, None, :]).reshape(k, n).astype(np.float32)
    by_word = np.ascontiguousarray(scaled.reshape(k // 512, 128, 4, n).transpose(0, 1, 3, 2))
    if fmt == "e4m3":
        words = by_word.astype(ml_dtypes.float8_e4m3fn).view(np.uint8)
    else:
        c = by_word.astype(ml_dtypes.float4_e2m1fn).view(np.uint8) & 0xF
        words = c[..., 0::2] | (c[..., 1::2] << 4)
    return np.ascontiguousarray(words), np.ascontiguousarray(byte.astype(np.uint8).reshape(k // 512, 16, n))


def unpack_weight(words, scales, fmt):
    g, p, n, _ = words.shape
    if fmt == "e4m3":
        vals = np.ascontiguousarray(words).view(ml_dtypes.float8_e4m3fn).astype(np.float64)
    else:
        nib = np.empty((g, p, n, 4), np.uint8)
        nib[..., 0::2] = words & 0xF
        nib[..., 1::2] = words >> 4
        vals = E2M1[nib]
    vals = vals * np.repeat(np.exp2(scales.astype(np.float64) - 127.0), 8, axis=1)[..., None]
    return vals.transpose(0, 1, 3, 2).reshape(g * 512, n)


B, I, H = 512, 1024, 1024
QH = H % 512 == 0
FMT = "e4m3"


def sigmoid(v):
    return 1.0 / (1.0 + np.exp(-v))


def setup_inputs():
    s = mx_kscale(I)
    t = mx_kscale(H) if QH else np.ones(H)
    n = np.random.standard_normal
    aw, ar = 0.6 / np.sqrt(I), 0.6 / np.sqrt(H)
    out = {"xt": bf(n((B, I)) * s), "cx": bf(n((B, H))), "hx": bf(n((B, H)) * t)}
    for name in ("w_fg", "w_ig", "w_og", "w_ci"):
        words, scales = pack_weight((n((H, I)) * aw / s).T, FMT)
        out[name + "_words"] = words
        out[name + "_scales"] = scales
    for name in ("r_fg", "r_ig", "r_og", "r_ci"):
        words, scales = pack_weight((n((H, H)) * ar / t).T, FMT)
        out[name + "_words"] = words
        out[name + "_scales"] = scales
    for name in ("b_fg", "b_ig", "b_og", "b_ci"):
        out[name] = bf(n(H) * 0.3)
    return out


def reference(xt, cx, hx, w_fg_words, w_fg_scales, w_ig_words, w_ig_scales, w_og_words, w_og_scales, w_ci_words, w_ci_scales,
              r_fg_words, r_fg_scales, r_ig_words, r_ig_scales, r_og_words, r_og_scales, r_ci_words, r_ci_scales,
              b_fg, b_ig, b_og, b_ci):
    W = np.concatenate([unpack_weight(w_fg_words, w_fg_scales, FMT), unpack_weight(w_ig_words, w_ig_scales, FMT),
                        unpack_weight(w_og_words, w_og_scales, FMT), unpack_weight(w_ci_words, w_ci_scales, FMT)], axis=1)
    R = np.concatenate([unpack_weight(r_fg_words, r_fg_scales, FMT), unpack_weight(r_ig_words, r_ig_scales, FMT),
                        unpack_weight(r_og_words, r_og_scales, FMT), unpack_weight(r_ci_words, r_ci_scales, FMT)], axis=1)
    b = np.concatenate([f64(b_fg), f64(b_ig), f64(b_og), f64(b_ci)], axis=0)
    gx = mxq(f64(xt), 1, "e4m3") @ W
    if QH:
        gh = mxq(f64(hx), 1, "e4m3") @ R
    else:
        gh = f64(hx) @ R
    gates = gx + gh + b
    f, i, o, g = np.split(gates, 4, axis=-1)
    ft = sigmoid(f)
    it = sigmoid(i)
    ot = sigmoid(o)
    ct = ft * f64(cx) + it * np.tanh(g)
    ht = ot * np.tanh(ct)
    return (ht, ct)

@@ -1,0 +1,216 @@
+from contextlib import ExitStack
+
+import concourse.mybir as mybir
+from concourse.masks import make_identity
+
+F32 = mybir.dt.float32
+BF16 = mybir.dt.bfloat16
+I32 = mybir.dt.int32
+U32 = mybir.dt.uint32
+U8 = mybir.dt.uint8
+FP8X4 = mybir.dt.float8_e4m3fn_x4
+ACT = mybir.ActivationFunctionType
+ALU = mybir.AluOpType
+
+P = 128
+PACK = 4
+K_PASS = P * PACK
+BATCH, HIDDEN = 512, 1024
+BATCH_TILES = BATCH // P
+PASSES = HIDDEN // K_PASS
+HALF = 512
+HALVES = HIDDEN // HALF
+PSUM_BANKS = 8
+QUADRANTS = 4
+GATES = ("f", "i", "g", "o")
+SOURCES = 2
+
+FLOPS = 2 * BATCH * (2 * HIDDEN) * (4 * HIDDEN)
+
+
+def tile_lstmcell_kernel(
+    tc, xt, cx, hx,
+    w_fg_words, w_fg_scales, w_ig_words, w_ig_scales, w_og_words, w_og_scales, w_ci_words, w_ci_scales,
+    r_fg_words, r_fg_scales, r_ig_words, r_ig_scales, r_og_words, r_og_scales, r_ci_words, r_ci_scales,
+    b_fg, b_ig, b_og, b_ci, out_0, out_1,
+):
+    nc = tc.nc
+    ht_out, ct_out = out_0, out_1
+    words_in = {
+        "f": (w_fg_words, r_fg_words), "i": (w_ig_words, r_ig_words),
+        "g": (w_ci_words, r_ci_words), "o": (w_og_words, r_og_words),
+    }
+    scales_in = {
+        "f": (w_fg_scales, r_fg_scales), "i": (w_ig_scales, r_ig_scales),
+        "g": (w_ci_scales, r_ci_scales), "o": (w_og_scales, r_og_scales),
+    }
+    bias_in = {"f": b_fg, "i": b_ig, "g": b_ci, "o": b_og}
+    gate_func = {"f": ACT.Sigmoid, "i": ACT.Sigmoid, "g": ACT.Tanh, "o": ACT.Sigmoid}
+
+    with ExitStack() as ctx:
+        keep = ctx.enter_context(tc.tile_pool(name="keep", bufs=1))
+        work = ctx.enter_context(tc.tile_pool(name="work", bufs=3))
+        psum = ctx.enter_context(tc.psum_pool(name="psum", bufs=PSUM_BANKS))
+        ctx.enter_context(tc.manual_schedule())
+
+        raw = {}
+        act_codes, act_planes = {}, {}
+        for bt in range(BATCH_TILES):
+            for s in range(SOURCES):
+                raw[(s, bt)] = keep.tile([P, HIDDEN], BF16, name="raw_%d_%d" % (s, bt))
+            act_codes[bt] = keep.tile([P, SOURCES, PASSES, P], U32, name="act_codes_%d" % bt, align_bytes=64)
+            act_planes[bt] = keep.tile([P, SOURCES, PASSES, P], U8, name="act_planes_%d" % bt, align_bytes=64)
+        w_words = {}
+        w_planes = {}
+        for gate in GATES:
+            w_planes[gate] = keep.tile([P, HIDDEN], U8, name="w_planes_%s" % gate, align_bytes=64)
+            for s in range(SOURCES):
+                for j in range(HALVES):
+                    w_words[(gate, s, j)] = keep.tile(
+                        [P, PASSES, HALF], I32, name="w_words_%s_%d_%d" % (gate, s, j), align_bytes=64
+                    )
+        cx_sb = [keep.tile([P, BATCH_TILES, HALF], BF16, name="cx_sb_%d" % j) for j in range(HALVES)]
+        bias_rows = keep.tile([P, len(GATES), HIDDEN], BF16, name="bias_rows")
+        bias_all = [keep.tile([P, len(GATES), HALF], F32, name="bias_all_%d" % j) for j in range(HALVES)]
+        ones = keep.tile([P, P], BF16, name="ones")
+        ident = keep.tile([P, P], F32, name="ident")
+        table_warm = keep.tile([P, 1], F32, name="table_warm")
+
+        for gate in GATES:
+            nc.vector.memset(w_planes[gate][:].bitcast(I32), 0)
+        nc.vector.memset(bias_rows[:].bitcast(I32), 0)
+        nc.vector.memset(ones[:], 1.0)
+        make_identity(nc, ident[:])
+        for n, gate in enumerate(GATES):
+            nc.scalar.dma_start(out=bias_rows[0:1, n, :], in_=bias_in[gate].rearrange("(o h) -> o h", o=1))
+        nc.scalar.activation(out=table_warm[:], in_=ones[:, 0:1], func=ACT.Sigmoid)
+
+        def load_scales(gate):
+            for s in range(SOURCES):
+                for quad in range(QUADRANTS):
+                    first = 32 * quad + 8 * s
+                    nc.sync.dma_start(
+                        out=w_planes[gate][first : first + 8, :].bitcast(I32),
+                        in_=scales_in[gate][s][:, 4 * quad : 4 * quad + 4, :].bitcast(I32),
+                    )
+
+        def load_words(gate, j):
+            for s in range(SOURCES):
+                by_partition = words_in[gate][s].rearrange("g p n t -> p g (n t)")
+                nc.sync.dma_start(
+                    out=w_words[(gate, s, j)][:],
+                    in_=by_partition[:, :, PACK * HALF * j : PACK * HALF * (j + 1)].bitcast(I32),
+                )
+
+        def load_cx(j):
+            nc.sync.dma_start(
+                out=cx_sb[j][:], in_=cx.rearrange("(t p) h -> p t h", p=P)[:, :, HALF * j : HALF * (j + 1)]
+            )
+
+        for bt in range(BATCH_TILES):
+            for s, source in enumerate((xt, hx)):
+                nc.sync.dma_start(out=raw[(s, bt)][:], in_=source[P * bt : P * (bt + 1), :])
+        for j in range(HALVES):
+            for gate in GATES:
+                if j == 0:
+                    load_scales(gate)
+                load_words(gate, j)
+                if gate == "f":
+                    load_cx(j)
+
+        def transpose_batch_tile(bt):
+            grouped = work.tile([P, SOURCES * PASSES * P * PACK], BF16, name="grouped", align_bytes=64)
+            for s in range(SOURCES):
+                pairs = raw[(s, bt)][:].bitcast(F32)
+                flipped = psum.tile([P, PASSES, 2, P], F32, name="flipped", tag="bank")
+                for g in range(PASSES):
+                    for u in range(2):
+                        nc.tensor.transpose(
+                            out=flipped[:, g, u, :],
+                            in_=pairs[:, 256 * g + u : 256 * (g + 1) : 2],
+                            identity=ident[:],
+                        )
+                width = PASSES * P * 2
+                side_by_side = grouped[:].bitcast(F32)[:, width * s : width * (s + 1)].rearrange(
+                    "p (g b u) -> p g b u", g=PASSES, u=2
+                )
+                if s == 0:
+                    nc.vector.tensor_copy(out=side_by_side, in_=flipped[:].rearrange("p g u b -> p g b u"))
+                else:
+                    nc.scalar.copy(out=side_by_side, in_=flipped[:].rearrange("p g u b -> p g b u"))
+            return grouped
+
+        def quantise_batch_tile(bt, grouped):
+            nc.vector.quantize_mx(
+                out=act_codes[bt][:].rearrange("p s g b -> p (s g b)").bitcast(FP8X4),
+                scales=act_planes[bt][:].rearrange("p s g b -> p (s g b)"),
+                in_=grouped[:],
+            )
+
+        waiting = None
+        for bt in range(BATCH_TILES):
+            grouped = transpose_batch_tile(bt)
+            if waiting is not None:
+                quantise_batch_tile(*waiting)
+            waiting = (bt, grouped)
+        quantise_batch_tile(*waiting)
+
+        def spread_biases(j):
+            for n in range(len(GATES)):
+                spread = psum.tile([P, HALF], F32, name="spread", tag="bank")
+                nc.tensor.matmul(
+                    out=spread[:], lhsT=ones[:], rhs=bias_rows[:, n, HALF * j : HALF * (j + 1)], start=True, stop=True
+                )
+                nc.scalar.copy(out=bias_all[j][:, n, :], in_=spread[:])
+
+        cell = {}
+
+        def gate_bank(j, gate, bt):
+            acc = psum.tile([P, HALF], F32, name="acc", tag="bank")
+            for s in range(SOURCES):
+                for g in range(PASSES):
+                    start_row = 8 * s + 4 * g
+                    nc.tensor.matmul_mx(
+                        out=acc[:],
+                        lhsT=act_codes[bt][:, s, g, :].bitcast(FP8X4),
+                        lhsT_scale=act_planes[bt][:, s, g, :],
+                        rhs=w_words[(gate, s, j)][:, g, :].bitcast(FP8X4),
+                        rhs_scale=w_planes[gate][start_row:P, HALF * j : HALF * (j + 1)],
+                        start=(s == 0 and g == 0),
+                        stop=(s == SOURCES - 1 and g == PASSES - 1),
+                    )
+            slots = {"f": HALVES * BATCH_TILES, "o": HALVES * BATCH_TILES, "i": BATCH_TILES + 1, "g": 3}
+            out = work.tile([P, HALF], F32, name="gate_%s" % gate, bufs=slots[gate])
+            nc.vector.tensor_tensor(out=out[:], in0=acc[:], in1=bias_all[j][:, GATES.index(gate), :], op=ALU.add)
+            nc.scalar.activation(out=out[:], in_=out[:], func=gate_func[gate])
+            cell[(gate, bt)] = out
+
+        def products(j, gate, bt):
+            rows = slice(P * bt, P * (bt + 1))
+            cols = slice(HALF * j, HALF * (j + 1))
+            if gate == "f":
+                f = cell[("f", bt)]
+                nc.vector.tensor_tensor(out=f[:], in0=f[:], in1=cx_sb[j][:, bt, :], op=ALU.mult)
+            if gate == "g":
+                i, ct = cell[("i", bt)], cell[("f", bt)]
+                nc.vector.tensor_tensor(out=i[:], in0=i[:], in1=cell[("g", bt)][:], op=ALU.mult)
+                nc.vector.tensor_tensor(out=ct[:], in0=ct[:], in1=i[:], op=ALU.add)
+                nc.sync.dma_start(out=ct_out[rows, cols], in_=ct[:])
+                tanh_ct = work.tile([P, HALF], F32, name="tanh_ct", bufs=BATCH_TILES + 1)
+                nc.scalar.activation(out=tanh_ct[:], in_=ct[:], func=ACT.Tanh)
+                cell[("tanh_ct", bt)] = tanh_ct
+            if gate == "o":
+                ht = cell[("o", bt)]
+                nc.vector.tensor_tensor(out=ht[:], in0=ht[:], in1=cell[("tanh_ct", bt)][:], op=ALU.mult)
+                nc.sync.dma_start(out=ht_out[rows, cols], in_=ht[:])
+
+        behind = None
+        for j in range(HALVES):
+            spread_biases(j)
+            for gate in GATES:
+                for bt in range(BATCH_TILES):
+                    gate_bank(j, gate, bt)
+                    if behind is not None:
+                        products(*behind)
+                    behind = (j, gate, bt)
+        products(*behind)

@@ -179,38 +179,40 @@ def tile_lstmcell_kernel(
                         start=(s == 0 and g == 0),
                         stop=(s == SOURCES - 1 and g == PASSES - 1),
                     )
-            slots = {"f": HALVES * BATCH_TILES, "o": HALVES * BATCH_TILES, "i": BATCH_TILES + 1, "g": 3}
+            slots = {"f": HALVES * BATCH_TILES, "o": HALVES * BATCH_TILES, "i": BATCH_TILES + 2, "g": 3}
             out = work.tile([P, HALF], F32, name="gate_%s" % gate, bufs=slots[gate])
             nc.vector.tensor_tensor(out=out[:], in0=acc[:], in1=bias_all[j][:, GATES.index(gate), :], op=ALU.add)
             nc.scalar.activation(out=out[:], in_=out[:], func=gate_func[gate])
             cell[(gate, bt)] = out
 
-        def products(j, gate, bt):
-            rows = slice(P * bt, P * (bt + 1))
-            cols = slice(HALF * j, HALF * (j + 1))
+        def multiply(j, gate, bt):
             if gate == "f":
                 f = cell[("f", bt)]
-                nc.vector.tensor_tensor(out=f[:], in0=f[:], in1=cx_sb[j][:, bt, :], op=ALU.mult)
+                nc.gpsimd.tensor_tensor(out=f[:], in0=f[:], in1=cx_sb[j][:, bt, :], op=ALU.mult)
             if gate == "g":
-                i, ct = cell[("i", bt)], cell[("f", bt)]
-                nc.vector.tensor_tensor(out=i[:], in0=i[:], in1=cell[("g", bt)][:], op=ALU.mult)
-                nc.vector.tensor_tensor(out=ct[:], in0=ct[:], in1=i[:], op=ALU.add)
-                nc.sync.dma_start(out=ct_out[rows, cols], in_=ct[:])
+                i = cell[("i", bt)]
+                nc.gpsimd.tensor_tensor(out=i[:], in0=i[:], in1=cell[("g", bt)][:], op=ALU.mult)
+            if gate == "o":
+                ht = cell[("o", bt)]
+                nc.gpsimd.tensor_tensor(out=ht[:], in0=ht[:], in1=cell[("tanh_ct", bt)][:], op=ALU.mult)
+                nc.sync.dma_start(out=ht_out[P * bt : P * (bt + 1), HALF * j : HALF * (j + 1)], in_=ht[:])
+
+        def finish_ct(j, gate, bt):
+            if gate == "g":
+                ct = cell[("f", bt)]
+                nc.vector.tensor_tensor(out=ct[:], in0=ct[:], in1=cell[("i", bt)][:], op=ALU.add)
+                nc.sync.dma_start(out=ct_out[P * bt : P * (bt + 1), HALF * j : HALF * (j + 1)], in_=ct[:])
                 tanh_ct = work.tile([P, HALF], F32, name="tanh_ct", bufs=BATCH_TILES + 1)
                 nc.scalar.activation(out=tanh_ct[:], in_=ct[:], func=ACT.Tanh)
                 cell[("tanh_ct", bt)] = tanh_ct
-            if gate == "o":
-                ht = cell[("o", bt)]
-                nc.vector.tensor_tensor(out=ht[:], in0=ht[:], in1=cell[("tanh_ct", bt)][:], op=ALU.mult)
-                nc.sync.dma_start(out=ht_out[rows, cols], in_=ht[:])
 
-        behind = None
-        for j in range(HALVES):
-            spread_biases(j)
-            for gate in GATES:
-                for bt in range(BATCH_TILES):
-                    gate_bank(j, gate, bt)
-                    if behind is not None:
-                        products(*behind)
-                    behind = (j, gate, bt)
-        products(*behind)
+        banks = [(j, gate, bt) for j in range(HALVES) for gate in GATES for bt in range(BATCH_TILES)]
+        for n in range(len(banks) + 2):
+            if n < len(banks):
+                if banks[n][1:] == (GATES[0], 0):
+                    spread_biases(banks[n][0])
+                gate_bank(*banks[n])
+            if 1 <= n <= len(banks):
+                multiply(*banks[n - 1])
+            if n >= 2:
+                finish_ct(*banks[n - 2])

@@ -24,6 +24,9 @@ PSUM_BANKS = 8
 QUADRANTS = 4
 GATES = ("f", "i", "g", "o")
 SOURCES = 2
+SUM_LAG = 3
+O_DELAY = 3
+CX_AFTER = ("f", "g")
 
 FLOPS = 2 * BATCH * (2 * HIDDEN) * (4 * HIDDEN)
 
@@ -63,44 +66,44 @@ def tile_lstmcell_kernel(
         w_words = {}
         w_planes = {}
         for gate in GATES:
-            w_planes[gate] = keep.tile([P, HIDDEN], U8, name="w_planes_%s" % gate, align_bytes=64)
             for s in range(SOURCES):
+                w_planes[(gate, s)] = keep.tile([P, HIDDEN], U8, name="w_planes_%s_%d" % (gate, s), align_bytes=64)
                 for j in range(HALVES):
                     w_words[(gate, s, j)] = keep.tile(
                         [P, PASSES, HALF], I32, name="w_words_%s_%d_%d" % (gate, s, j), align_bytes=64
                     )
         cx_sb = [keep.tile([P, BATCH_TILES, HALF], BF16, name="cx_sb_%d" % j) for j in range(HALVES)]
-        bias_rows = keep.tile([P, len(GATES), HIDDEN], BF16, name="bias_rows")
-        bias_all = [keep.tile([P, len(GATES), HALF], F32, name="bias_all_%d" % j) for j in range(HALVES)]
-        ones = keep.tile([P, P], BF16, name="ones")
-        ident = keep.tile([P, P], F32, name="ident")
-        table_warm = keep.tile([P, 1], F32, name="table_warm")
-
+        bias_rows = keep.tile([P, HALF], BF16, name="bias_rows")
+        bias_all = {}
         for gate in GATES:
-            nc.vector.memset(w_planes[gate][:].bitcast(I32), 0)
+            bias_all[gate] = keep.tile([P, HIDDEN], BF16, name="bias_all_%s" % gate)
+        ident = keep.tile([P, P], F32, name="ident")
+        ident_bf = keep.tile([P, P], BF16, name="ident_bf")
+        table_warm = keep.tile([P, 2], F32, name="table_warm")
+
+        nc.vector.memset(table_warm[:], 0.0)
         nc.vector.memset(bias_rows[:].bitcast(I32), 0)
-        nc.vector.memset(ones[:], 1.0)
+        nc.scalar.activation(out=table_warm[:, 1:2], in_=table_warm[:, 0:1], func=ACT.Sigmoid)
         make_identity(nc, ident[:])
-        for n, gate in enumerate(GATES):
-            nc.scalar.dma_start(out=bias_rows[0:1, n, :], in_=bias_in[gate].rearrange("(o h) -> o h", o=1))
-        nc.scalar.activation(out=table_warm[:], in_=ones[:, 0:1], func=ACT.Sigmoid)
-
-        def load_scales(gate):
+        for gate in GATES:
             for s in range(SOURCES):
-                for quad in range(QUADRANTS):
-                    first = 32 * quad + 8 * s
-                    nc.sync.dma_start(
-                        out=w_planes[gate][first : first + 8, :].bitcast(I32),
-                        in_=scales_in[gate][s][:, 4 * quad : 4 * quad + 4, :].bitcast(I32),
-                    )
+                nc.vector.memset(w_planes[(gate, s)][:].bitcast(I32), 0)
+        nc.vector.tensor_copy(out=ident_bf[:], in_=ident[:])
 
-        def load_words(gate, j):
-            for s in range(SOURCES):
-                by_partition = words_in[gate][s].rearrange("g p n t -> p g (n t)")
+        def load_scales(gate, s):
+            for quad in range(QUADRANTS):
+                first = 32 * quad + 8 * s
                 nc.sync.dma_start(
-                    out=w_words[(gate, s, j)][:],
-                    in_=by_partition[:, :, PACK * HALF * j : PACK * HALF * (j + 1)].bitcast(I32),
+                    out=w_planes[(gate, s)][first : first + 8, :].bitcast(I32),
+                    in_=scales_in[gate][s][:, 4 * quad : 4 * quad + 4, :].bitcast(I32),
                 )
+
+        def load_words(gate, s, j):
+            by_partition = words_in[gate][s].rearrange("g p n t -> p g (n t)")
+            nc.sync.dma_start(
+                out=w_words[(gate, s, j)][:],
+                in_=by_partition[:, :, PACK * HALF * j : PACK * HALF * (j + 1)].bitcast(I32),
+            )
 
         def load_cx(j):
             nc.sync.dma_start(
@@ -110,12 +113,19 @@ def tile_lstmcell_kernel(
         for bt in range(BATCH_TILES):
             for s, source in enumerate((xt, hx)):
                 nc.sync.dma_start(out=raw[(s, bt)][:], in_=source[P * bt : P * (bt + 1), :])
+            if bt == 0:
+                for n, gate in enumerate(GATES):
+                    nc.sync.dma_start(
+                        out=bias_rows[HALVES * n : HALVES * (n + 1), :],
+                        in_=bias_in[gate].rearrange("(j h) -> j h", j=HALVES),
+                    )
         for j in range(HALVES):
             for gate in GATES:
-                if j == 0:
-                    load_scales(gate)
-                load_words(gate, j)
-                if gate == "f":
+                for s in range(SOURCES):
+                    if j == 0:
+                        load_scales(gate, s)
+                    load_words(gate, s, j)
+                if gate == CX_AFTER[j]:
                     load_cx(j)
 
         def transpose_batch_tile(bt):
@@ -141,78 +151,117 @@ def tile_lstmcell_kernel(
             return grouped
 
         def quantise_batch_tile(bt, grouped):
-            nc.vector.quantize_mx(
-                out=act_codes[bt][:].rearrange("p s g b -> p (s g b)").bitcast(FP8X4),
-                scales=act_planes[bt][:].rearrange("p s g b -> p (s g b)"),
-                in_=grouped[:],
-            )
+            width = PASSES * P * PACK
+            for s in range(SOURCES):
+                nc.vector.quantize_mx(
+                    out=act_codes[bt][:, s, :, :].rearrange("p g b -> p (g b)").bitcast(FP8X4),
+                    scales=act_planes[bt][:, s, :, :].rearrange("p g b -> p (g b)"),
+                    in_=grouped[:, width * s : width * (s + 1)],
+                )
+
+        def spread_bias(n):
+            spread = psum.tile([P, HIDDEN], BF16, name="spread", tag="bank")
+            for j in range(HALVES):
+                r = HALVES * n + j
+                nc.tensor.matmul(
+                    out=spread[:, HALF * j : HALF * (j + 1)],
+                    lhsT=ident_bf[:, r : r + 1].to_broadcast([P, P]),
+                    rhs=bias_rows[:],
+                    start=True,
+                    stop=True,
+                )
+            return spread
 
         waiting = None
+        spreads = []
         for bt in range(BATCH_TILES):
             grouped = transpose_batch_tile(bt)
+            spreads.append(spread_bias(bt))
+            if bt < BATCH_TILES // 2:
+                nc.scalar.copy(out=bias_all[GATES[bt]][:], in_=spreads[bt][:])
             if waiting is not None:
                 quantise_batch_tile(*waiting)
             waiting = (bt, grouped)
+        for bt in range(BATCH_TILES // 2, BATCH_TILES):
+            nc.scalar.copy(out=bias_all[GATES[bt]][:], in_=spreads[bt][:])
         quantise_batch_tile(*waiting)
 
-        def spread_biases(j):
-            for n in range(len(GATES)):
-                spread = psum.tile([P, HALF], F32, name="spread", tag="bank")
-                nc.tensor.matmul(
-                    out=spread[:], lhsT=ones[:], rhs=bias_rows[:, n, HALF * j : HALF * (j + 1)], start=True, stop=True
-                )
-                nc.scalar.copy(out=bias_all[j][:, n, :], in_=spread[:])
-
         cell = {}
+        open_banks = {}
 
-        def gate_bank(j, gate, bt):
-            acc = psum.tile([P, HALF], F32, name="acc", tag="bank")
-            for s in range(SOURCES):
-                for g in range(PASSES):
-                    start_row = 8 * s + 4 * g
-                    nc.tensor.matmul_mx(
-                        out=acc[:],
-                        lhsT=act_codes[bt][:, s, g, :].bitcast(FP8X4),
-                        lhsT_scale=act_planes[bt][:, s, g, :],
-                        rhs=w_words[(gate, s, j)][:, g, :].bitcast(FP8X4),
-                        rhs_scale=w_planes[gate][start_row:P, HALF * j : HALF * (j + 1)],
-                        start=(s == 0 and g == 0),
-                        stop=(s == SOURCES - 1 and g == PASSES - 1),
-                    )
-            slots = {"f": HALVES * BATCH_TILES, "o": HALVES * BATCH_TILES, "i": BATCH_TILES + 2, "g": 3}
+        def mx_passes(j, gate, bt, s):
+            if s == 0:
+                open_banks[bt] = psum.tile([P, HALF], F32, name="acc", tag="bank")
+            for g in range(PASSES):
+                start_row = 8 * s + 4 * g
+                nc.tensor.matmul_mx(
+                    out=open_banks[bt][:],
+                    lhsT=act_codes[bt][:, s, g, :].bitcast(FP8X4),
+                    lhsT_scale=act_planes[bt][:, s, g, :],
+                    rhs=w_words[(gate, s, j)][:, g, :].bitcast(FP8X4),
+                    rhs_scale=w_planes[(gate, s)][start_row:P, HALF * j : HALF * (j + 1)],
+                    start=(s == 0 and g == 0),
+                    stop=(s == SOURCES - 1 and g == PASSES - 1),
+                )
+
+        def empty_bank(j, gate, bt):
+            slots = {"f": HALVES * BATCH_TILES, "o": HALVES * BATCH_TILES, "i": BATCH_TILES + 3, "g": 4}
             out = work.tile([P, HALF], F32, name="gate_%s" % gate, bufs=slots[gate])
-            nc.vector.tensor_tensor(out=out[:], in0=acc[:], in1=bias_all[j][:, GATES.index(gate), :], op=ALU.add)
+            nc.vector.tensor_tensor(
+                out=out[:], in0=open_banks[bt][:], in1=bias_all[gate][:, HALF * j : HALF * (j + 1)], op=ALU.add
+            )
             nc.scalar.activation(out=out[:], in_=out[:], func=gate_func[gate])
-            cell[(gate, bt)] = out
+            cell[(gate, j, bt)] = out
 
-        def multiply(j, gate, bt):
-            if gate == "f":
-                f = cell[("f", bt)]
-                nc.gpsimd.tensor_tensor(out=f[:], in0=f[:], in1=cx_sb[j][:, bt, :], op=ALU.mult)
-            if gate == "g":
-                i = cell[("i", bt)]
-                nc.gpsimd.tensor_tensor(out=i[:], in0=i[:], in1=cell[("g", bt)][:], op=ALU.mult)
-            if gate == "o":
-                ht = cell[("o", bt)]
-                nc.gpsimd.tensor_tensor(out=ht[:], in0=ht[:], in1=cell[("tanh_ct", bt)][:], op=ALU.mult)
-                nc.sync.dma_start(out=ht_out[P * bt : P * (bt + 1), HALF * j : HALF * (j + 1)], in_=ht[:])
+        later = {}
 
-        def finish_ct(j, gate, bt):
-            if gate == "g":
-                ct = cell[("f", bt)]
-                nc.vector.tensor_tensor(out=ct[:], in0=ct[:], in1=cell[("i", bt)][:], op=ALU.add)
-                nc.sync.dma_start(out=ct_out[P * bt : P * (bt + 1), HALF * j : HALF * (j + 1)], in_=ct[:])
-                tanh_ct = work.tile([P, HALF], F32, name="tanh_ct", bufs=BATCH_TILES + 1)
-                nc.scalar.activation(out=tanh_ct[:], in_=ct[:], func=ACT.Tanh)
-                cell[("tanh_ct", bt)] = tanh_ct
+        def at_step(n, what, j, bt):
+            later.setdefault(n, []).append((what, j, bt))
 
-        banks = [(j, gate, bt) for j in range(HALVES) for gate in GATES for bt in range(BATCH_TILES)]
-        for n in range(len(banks) + 2):
+        def times_cx(j, bt):
+            f = cell[("f", j, bt)]
+            nc.gpsimd.tensor_tensor(out=f[:], in0=f[:], in1=cx_sb[j][:, bt, :], op=ALU.mult)
+
+        def i_times_g(j, bt):
+            i = cell[("i", j, bt)]
+            nc.gpsimd.tensor_tensor(out=i[:], in0=i[:], in1=cell[("g", j, bt)][:], op=ALU.mult)
+
+        def finish_ct(j, bt):
+            ct = cell[("f", j, bt)]
+            nc.vector.tensor_tensor(out=ct[:], in0=ct[:], in1=cell[("i", j, bt)][:], op=ALU.add)
+            nc.sync.dma_start(out=ct_out[P * bt : P * (bt + 1), HALF * j : HALF * (j + 1)], in_=ct[:])
+            tanh_ct = work.tile([P, HALF], F32, name="tanh_ct", bufs=BATCH_TILES + 1)
+            nc.scalar.activation(out=tanh_ct[:], in_=ct[:], func=ACT.Tanh)
+            cell[("tanh_ct", j, bt)] = tanh_ct
+
+        def finish_ht(j, bt):
+            ht = cell[("o", j, bt)]
+            engine = nc.gpsimd if bt < BATCH_TILES // 2 else nc.vector
+            engine.tensor_tensor(out=ht[:], in0=ht[:], in1=cell[("tanh_ct", j, bt)][:], op=ALU.mult)
+            nc.sync.dma_start(out=ht_out[P * bt : P * (bt + 1), HALF * j : HALF * (j + 1)], in_=ht[:])
+
+        banks = [(0, gate, bt) for gate in GATES for bt in range(BATCH_TILES)]
+        for bt in range(BATCH_TILES + O_DELAY):
+            if bt < BATCH_TILES:
+                banks.extend((1, gate, bt) for gate in GATES[:3])
+            if bt >= O_DELAY:
+                banks.append((1, GATES[3], bt - O_DELAY))
+        for n in range(len(banks) + SUM_LAG):
+            if n == 0:
+                for m in range(BATCH_TILES):
+                    mx_passes(*banks[m], 0)
             if n < len(banks):
-                if banks[n][1:] == (GATES[0], 0):
-                    spread_biases(banks[n][0])
-                gate_bank(*banks[n])
-            if 1 <= n <= len(banks):
-                multiply(*banks[n - 1])
-            if n >= 2:
-                finish_ct(*banks[n - 2])
+                j, gate, bt = banks[n]
+                if n >= BATCH_TILES:
+                    mx_passes(j, gate, bt, 0)
+                mx_passes(j, gate, bt, 1)
+                empty_bank(j, gate, bt)
+                if gate == "f":
+                    at_step(n + 1, times_cx, j, bt)
+                if gate == "g":
+                    at_step(n + 1, i_times_g, j, bt)
+                    at_step(n + SUM_LAG, finish_ct, j, bt)
+                if gate == "o":
+                    at_step(n + 1, finish_ht, j, bt)
+            for what, j, bt in later.get(n, []):
+                what(j, bt)

@@ -25,8 +25,7 @@ QUADRANTS = 4
 GATES = ("f", "i", "g", "o")
 SOURCES = 2
 SUM_LAG = 3
-O_DELAY = 3
-CX_AFTER = ("f", "g")
+CX_AFTER = ("f", "f")
 
 FLOPS = 2 * BATCH * (2 * HIDDEN) * (4 * HIDDEN)
 
@@ -241,11 +240,10 @@ def tile_lstmcell_kernel(
             nc.sync.dma_start(out=ht_out[P * bt : P * (bt + 1), HALF * j : HALF * (j + 1)], in_=ht[:])
 
         banks = [(0, gate, bt) for gate in GATES for bt in range(BATCH_TILES)]
-        for bt in range(BATCH_TILES + O_DELAY):
-            if bt < BATCH_TILES:
-                banks.extend((1, gate, bt) for gate in GATES[:3])
-            if bt >= O_DELAY:
-                banks.append((1, GATES[3], bt - O_DELAY))
+        banks.extend((1, "f", bt) for bt in range(BATCH_TILES))
+        for bt in range(BATCH_TILES):
+            banks.extend((1, gate, bt) for gate in ("i", "g"))
+        banks.extend((1, "o", bt) for bt in range(BATCH_TILES))
         for n in range(len(banks) + SUM_LAG):
             if n == 0:
                 for m in range(BATCH_TILES):

@@ -25,6 +25,7 @@ QUADRANTS = 4
 GATES = ("f", "i", "g", "o")
 SOURCES = 2
 SUM_LAG = 3
+PROBE = 8
 CX_AFTER = ("f", "f")
 
 FLOPS = 2 * BATCH * (2 * HIDDEN) * (4 * HIDDEN)
@@ -79,6 +80,7 @@ def tile_lstmcell_kernel(
         ident = keep.tile([P, P], F32, name="ident")
         ident_bf = keep.tile([P, P], BF16, name="ident_bf")
         table_warm = keep.tile([P, 2], F32, name="table_warm")
+        zeros = keep.tile([P, HALF], BF16, name="zeros")
 
         nc.vector.memset(table_warm[:], 0.0)
         nc.vector.memset(bias_rows[:].bitcast(I32), 0)
@@ -88,6 +90,7 @@ def tile_lstmcell_kernel(
             for s in range(SOURCES):
                 nc.vector.memset(w_planes[(gate, s)][:].bitcast(I32), 0)
         nc.vector.tensor_copy(out=ident_bf[:], in_=ident[:])
+        nc.vector.memset(zeros[:].bitcast(I32), 0)
 
         def load_scales(gate, s):
             for quad in range(QUADRANTS):
@@ -184,6 +187,10 @@ def tile_lstmcell_kernel(
         for bt in range(BATCH_TILES // 2, BATCH_TILES):
             nc.scalar.copy(out=bias_all[GATES[bt]][:], in_=spreads[bt][:])
         quantise_batch_tile(*waiting)
+
+        for n in range(PROBE):
+            idle = psum.tile([P, HALF], F32, name="idle", tag="bank")
+            nc.tensor.matmul(out=idle[:], lhsT=zeros[:, 0:P], rhs=zeros[:], start=True, stop=True)
 
         cell = {}
         open_banks = {}

@@ -25,7 +25,6 @@ QUADRANTS = 4
 GATES = ("f", "i", "g", "o")
 SOURCES = 2
 SUM_LAG = 3
-PROBE = 8
 CX_AFTER = ("f", "f")
 
 FLOPS = 2 * BATCH * (2 * HIDDEN) * (4 * HIDDEN)
@@ -80,7 +79,6 @@ def tile_lstmcell_kernel(
         ident = keep.tile([P, P], F32, name="ident")
         ident_bf = keep.tile([P, P], BF16, name="ident_bf")
         table_warm = keep.tile([P, 2], F32, name="table_warm")
-        zeros = keep.tile([P, HALF], BF16, name="zeros")
 
         nc.vector.memset(table_warm[:], 0.0)
         nc.vector.memset(bias_rows[:].bitcast(I32), 0)
@@ -90,7 +88,6 @@ def tile_lstmcell_kernel(
             for s in range(SOURCES):
                 nc.vector.memset(w_planes[(gate, s)][:].bitcast(I32), 0)
         nc.vector.tensor_copy(out=ident_bf[:], in_=ident[:])
-        nc.vector.memset(zeros[:].bitcast(I32), 0)
 
         def load_scales(gate, s):
             for quad in range(QUADRANTS):
@@ -188,10 +185,6 @@ def tile_lstmcell_kernel(
             nc.scalar.copy(out=bias_all[GATES[bt]][:], in_=spreads[bt][:])
         quantise_batch_tile(*waiting)
 
-        for n in range(PROBE):
-            idle = psum.tile([P, HALF], F32, name="idle", tag="bank")
-            nc.tensor.matmul(out=idle[:], lhsT=zeros[:, 0:P], rhs=zeros[:], start=True, stop=True)
-
         cell = {}
         open_banks = {}
 
@@ -224,13 +217,16 @@ def tile_lstmcell_kernel(
         def at_step(n, what, j, bt):
             later.setdefault(n, []).append((what, j, bt))
 
+        def product_engine(bt):
+            return nc.vector if bt % 2 else nc.gpsimd
+
         def times_cx(j, bt):
             f = cell[("f", j, bt)]
-            nc.gpsimd.tensor_tensor(out=f[:], in0=f[:], in1=cx_sb[j][:, bt, :], op=ALU.mult)
+            product_engine(bt).tensor_tensor(out=f[:], in0=f[:], in1=cx_sb[j][:, bt, :], op=ALU.mult)
 
         def i_times_g(j, bt):
             i = cell[("i", j, bt)]
-            nc.gpsimd.tensor_tensor(out=i[:], in0=i[:], in1=cell[("g", j, bt)][:], op=ALU.mult)
+            product_engine(bt).tensor_tensor(out=i[:], in0=i[:], in1=cell[("g", j, bt)][:], op=ALU.mult)
 
         def finish_ct(j, bt):
             ct = cell[("f", j, bt)]
@@ -242,8 +238,7 @@ def tile_lstmcell_kernel(
 
         def finish_ht(j, bt):
             ht = cell[("o", j, bt)]
-            engine = nc.gpsimd if bt < BATCH_TILES // 2 else nc.vector
-            engine.tensor_tensor(out=ht[:], in0=ht[:], in1=cell[("tanh_ct", j, bt)][:], op=ALU.mult)
+            product_engine(bt).tensor_tensor(out=ht[:], in0=ht[:], in1=cell[("tanh_ct", j, bt)][:], op=ALU.mult)
             nc.sync.dma_start(out=ht_out[P * bt : P * (bt + 1), HALF * j : HALF * (j + 1)], in_=ht[:])
 
         banks = [(0, gate, bt) for gate in GATES for bt in range(BATCH_TILES)]

from contextlib import ExitStack

import concourse.mybir as mybir
from concourse.masks import make_identity

F32 = mybir.dt.float32
BF16 = mybir.dt.bfloat16
I32 = mybir.dt.int32
U32 = mybir.dt.uint32
U8 = mybir.dt.uint8
FP8X4 = mybir.dt.float8_e4m3fn_x4
ACT = mybir.ActivationFunctionType
ALU = mybir.AluOpType

P = 128
PACK = 4
K_PASS = P * PACK
BATCH, HIDDEN = 512, 1024
BATCH_TILES = BATCH // P
PASSES = HIDDEN // K_PASS
HALF = 512
HALVES = HIDDEN // HALF
PSUM_BANKS = 8
QUADRANTS = 4
GATES = ("f", "i", "g", "o")
SOURCES = 2
SUM_LAG = 3
CX_AFTER = ("f", "f")

FLOPS = 2 * BATCH * (2 * HIDDEN) * (4 * HIDDEN)


def tile_lstmcell_kernel(
    tc, xt, cx, hx,
    w_fg_words, w_fg_scales, w_ig_words, w_ig_scales, w_og_words, w_og_scales, w_ci_words, w_ci_scales,
    r_fg_words, r_fg_scales, r_ig_words, r_ig_scales, r_og_words, r_og_scales, r_ci_words, r_ci_scales,
    b_fg, b_ig, b_og, b_ci, out_0, out_1,
):
    nc = tc.nc
    ht_out, ct_out = out_0, out_1
    words_in = {
        "f": (w_fg_words, r_fg_words), "i": (w_ig_words, r_ig_words),
        "g": (w_ci_words, r_ci_words), "o": (w_og_words, r_og_words),
    }
    scales_in = {
        "f": (w_fg_scales, r_fg_scales), "i": (w_ig_scales, r_ig_scales),
        "g": (w_ci_scales, r_ci_scales), "o": (w_og_scales, r_og_scales),
    }
    bias_in = {"f": b_fg, "i": b_ig, "g": b_ci, "o": b_og}
    gate_func = {"f": ACT.Sigmoid, "i": ACT.Sigmoid, "g": ACT.Tanh, "o": ACT.Sigmoid}

    with ExitStack() as ctx:
        keep = ctx.enter_context(tc.tile_pool(name="keep", bufs=1))
        work = ctx.enter_context(tc.tile_pool(name="work", bufs=3))
        psum = ctx.enter_context(tc.psum_pool(name="psum", bufs=PSUM_BANKS))
        ctx.enter_context(tc.manual_schedule())

        raw = {}
        act_codes, act_planes = {}, {}
        for bt in range(BATCH_TILES):
            for s in range(SOURCES):
                raw[(s, bt)] = keep.tile([P, HIDDEN], BF16, name="raw_%d_%d" % (s, bt))
            act_codes[bt] = keep.tile([P, SOURCES, PASSES, P], U32, name="act_codes_%d" % bt, align_bytes=64)
            act_planes[bt] = keep.tile([P, SOURCES, PASSES, P], U8, name="act_planes_%d" % bt, align_bytes=64)
        w_words = {}
        w_planes = {}
        for gate in GATES:
            for s in range(SOURCES):
                w_planes[(gate, s)] = keep.tile([P, HIDDEN], U8, name="w_planes_%s_%d" % (gate, s), align_bytes=64)
                for j in range(HALVES):
                    w_words[(gate, s, j)] = keep.tile(
                        [P, PASSES, HALF], I32, name="w_words_%s_%d_%d" % (gate, s, j), align_bytes=64
                    )
        cx_sb = [keep.tile([P, BATCH_TILES, HALF], BF16, name="cx_sb_%d" % j) for j in range(HALVES)]
        bias_rows = keep.tile([P, HALF], BF16, name="bias_rows")
        bias_all = {}
        for gate in GATES:
            bias_all[gate] = keep.tile([P, HIDDEN], BF16, name="bias_all_%s" % gate)
        ident = keep.tile([P, P], F32, name="ident")
        ident_bf = keep.tile([P, P], BF16, name="ident_bf")
        table_warm = keep.tile([P, 2], F32, name="table_warm")

        nc.vector.memset(table_warm[:], 0.0)
        nc.vector.memset(bias_rows[:].bitcast(I32), 0)
        nc.scalar.activation(out=table_warm[:, 1:2], in_=table_warm[:, 0:1], func=ACT.Sigmoid)
        make_identity(nc, ident[:])
        for gate in GATES:
            for s in range(SOURCES):
                nc.vector.memset(w_planes[(gate, s)][:].bitcast(I32), 0)
        nc.vector.tensor_copy(out=ident_bf[:], in_=ident[:])

        def load_scales(gate, s):
            for quad in range(QUADRANTS):
                first = 32 * quad + 8 * s
                nc.sync.dma_start(
                    out=w_planes[(gate, s)][first : first + 8, :].bitcast(I32),
                    in_=scales_in[gate][s][:, 4 * quad : 4 * quad + 4, :].bitcast(I32),
                )

        def load_words(gate, s, j):
            by_partition = words_in[gate][s].rearrange("g p n t -> p g (n t)")
            nc.sync.dma_start(
                out=w_words[(gate, s, j)][:],
                in_=by_partition[:, :, PACK * HALF * j : PACK * HALF * (j + 1)].bitcast(I32),
            )

        def load_cx(j):
            nc.sync.dma_start(
                out=cx_sb[j][:], in_=cx.rearrange("(t p) h -> p t h", p=P)[:, :, HALF * j : HALF * (j + 1)]
            )

        for bt in range(BATCH_TILES):
            for s, source in enumerate((xt, hx)):
                nc.sync.dma_start(out=raw[(s, bt)][:], in_=source[P * bt : P * (bt + 1), :])
            if bt == 0:
                for n, gate in enumerate(GATES):
                    nc.sync.dma_start(
                        out=bias_rows[HALVES * n : HALVES * (n + 1), :],
                        in_=bias_in[gate].rearrange("(j h) -> j h", j=HALVES),
                    )
        for j in range(HALVES):
            for gate in GATES:
                for s in range(SOURCES):
                    if j == 0:
                        load_scales(gate, s)
                    load_words(gate, s, j)
                if gate == CX_AFTER[j]:
                    load_cx(j)

        def transpose_batch_tile(bt):
            grouped = work.tile([P, SOURCES * PASSES * P * PACK], BF16, name="grouped", align_bytes=64)
            for s in range(SOURCES):
                pairs = raw[(s, bt)][:].bitcast(F32)
                flipped = psum.tile([P, PASSES, 2, P], F32, name="flipped", tag="bank")
                for g in range(PASSES):
                    for u in range(2):
                        nc.tensor.transpose(
                            out=flipped[:, g, u, :],
                            in_=pairs[:, 256 * g + u : 256 * (g + 1) : 2],
                            identity=ident[:],
                        )
                width = PASSES * P * 2
                side_by_side = grouped[:].bitcast(F32)[:, width * s : width * (s + 1)].rearrange(
                    "p (g b u) -> p g b u", g=PASSES, u=2
                )
                if s == 0:
                    nc.vector.tensor_copy(out=side_by_side, in_=flipped[:].rearrange("p g u b -> p g b u"))
                else:
                    nc.scalar.copy(out=side_by_side, in_=flipped[:].rearrange("p g u b -> p g b u"))
            return grouped

        def quantise_batch_tile(bt, grouped):
            width = PASSES * P * PACK
            for s in range(SOURCES):
                nc.vector.quantize_mx(
                    out=act_codes[bt][:, s, :, :].rearrange("p g b -> p (g b)").bitcast(FP8X4),
                    scales=act_planes[bt][:, s, :, :].rearrange("p g b -> p (g b)"),
                    in_=grouped[:, width * s : width * (s + 1)],
                )

        def spread_bias(n):
            spread = psum.tile([P, HIDDEN], BF16, name="spread", tag="bank")
            for j in range(HALVES):
                r = HALVES * n + j
                nc.tensor.matmul(
                    out=spread[:, HALF * j : HALF * (j + 1)],
                    lhsT=ident_bf[:, r : r + 1].to_broadcast([P, P]),
                    rhs=bias_rows[:],
                    start=True,
                    stop=True,
                )
            return spread

        waiting = None
        spreads = []
        for bt in range(BATCH_TILES):
            grouped = transpose_batch_tile(bt)
            spreads.append(spread_bias(bt))
            if bt < BATCH_TILES // 2:
                nc.scalar.copy(out=bias_all[GATES[bt]][:], in_=spreads[bt][:])
            if waiting is not None:
                quantise_batch_tile(*waiting)
            waiting = (bt, grouped)
        for bt in range(BATCH_TILES // 2, BATCH_TILES):
            nc.scalar.copy(out=bias_all[GATES[bt]][:], in_=spreads[bt][:])
        quantise_batch_tile(*waiting)

        cell = {}
        open_banks = {}

        def mx_passes(j, gate, bt, s):
            if s == 0:
                open_banks[bt] = psum.tile([P, HALF], F32, name="acc", tag="bank")
            for g in range(PASSES):
                start_row = 8 * s + 4 * g
                nc.tensor.matmul_mx(
                    out=open_banks[bt][:],
                    lhsT=act_codes[bt][:, s, g, :].bitcast(FP8X4),
                    lhsT_scale=act_planes[bt][:, s, g, :],
                    rhs=w_words[(gate, s, j)][:, g, :].bitcast(FP8X4),
                    rhs_scale=w_planes[(gate, s)][start_row:P, HALF * j : HALF * (j + 1)],
                    start=(s == 0 and g == 0),
                    stop=(s == SOURCES - 1 and g == PASSES - 1),
                )

        def empty_bank(j, gate, bt):
            slots = {"f": HALVES * BATCH_TILES, "o": HALVES * BATCH_TILES, "i": BATCH_TILES + 3, "g": 4}
            out = work.tile([P, HALF], F32, name="gate_%s" % gate, bufs=slots[gate])
            nc.vector.tensor_tensor(
                out=out[:], in0=open_banks[bt][:], in1=bias_all[gate][:, HALF * j : HALF * (j + 1)], op=ALU.add
            )
            nc.scalar.activation(out=out[:], in_=out[:], func=gate_func[gate])
            cell[(gate, j, bt)] = out

        later = {}

        def at_step(n, what, j, bt):
            later.setdefault(n, []).append((what, j, bt))

        def product_engine(bt):
            return nc.vector if bt % 2 else nc.gpsimd

        def times_cx(j, bt):
            f = cell[("f", j, bt)]
            product_engine(bt).tensor_tensor(out=f[:], in0=f[:], in1=cx_sb[j][:, bt, :], op=ALU.mult)

        def i_times_g(j, bt):
            i = cell[("i", j, bt)]
            product_engine(bt).tensor_tensor(out=i[:], in0=i[:], in1=cell[("g", j, bt)][:], op=ALU.mult)

        def finish_ct(j, bt):
            ct = cell[("f", j, bt)]
            nc.vector.tensor_tensor(out=ct[:], in0=ct[:], in1=cell[("i", j, bt)][:], op=ALU.add)
            nc.sync.dma_start(out=ct_out[P * bt : P * (bt + 1), HALF * j : HALF * (j + 1)], in_=ct[:])
            tanh_ct = work.tile([P, HALF], F32, name="tanh_ct", bufs=BATCH_TILES + 1)
            nc.scalar.activation(out=tanh_ct[:], in_=ct[:], func=ACT.Tanh)
            cell[("tanh_ct", j, bt)] = tanh_ct

        def finish_ht(j, bt):
            ht = cell[("o", j, bt)]
            product_engine(bt).tensor_tensor(out=ht[:], in0=ht[:], in1=cell[("tanh_ct", j, bt)][:], op=ALU.mult)
            nc.sync.dma_start(out=ht_out[P * bt : P * (bt + 1), HALF * j : HALF * (j + 1)], in_=ht[:])

        banks = [(0, gate, bt) for gate in GATES for bt in range(BATCH_TILES)]
        banks.extend((1, "f", bt) for bt in range(BATCH_TILES))
        for bt in range(BATCH_TILES):
            banks.extend((1, gate, bt) for gate in ("i", "g"))
        banks.extend((1, "o", bt) for bt in range(BATCH_TILES))
        for n in range(len(banks) + SUM_LAG):
            if n == 0:
                for m in range(BATCH_TILES):
                    mx_passes(*banks[m], 0)
            if n < len(banks):
                j, gate, bt = banks[n]
                if n >= BATCH_TILES:
                    mx_passes(j, gate, bt, 0)
                mx_passes(j, gate, bt, 1)
                empty_bank(j, gate, bt)
                if gate == "f":
                    at_step(n + 1, times_cx, j, bt)
                if gate == "g":
                    at_step(n + 1, i_times_g, j, bt)
                    at_step(n + SUM_LAG, finish_ct, j, bt)
                if gate == "o":
                    at_step(n + 1, finish_ht, j, bt)
            for what, j, bt in later.get(n, []):
                what(j, bt)
